import numpy as np
import ml_dtypes

BF16 = ml_dtypes.bfloat16


def bf(x):
    return np.asarray(x, np.float32).astype(BF16)


def f32(x):
    return np.asarray(x, np.float32)


def f64(x):
    return np.asarray(x).astype(np.float64)


def striped(idx):
    return np.tile(idx.reshape(-1, 16).T, (8, 1))


V, D, H1, H2, N = 256, 128, 512, 256, 1024


def setup_inputs():
    return {"table": bf(np.random.standard_normal((V, D))), "w1": bf(np.random.standard_normal((D, H1)) / np.sqrt(D)), "b1": f32(0.1 * np.random.standard_normal((H1, 1))), "w2": bf(np.random.standard_normal((H1, H2)) * np.sqrt(2.0 / H1)), "b2": f32(0.1 * np.random.standard_normal((H2, 1))), "w_out": bf(np.random.standard_normal((H2, V)) * np.sqrt(2.0 / H2)), "b_out": f32(0.1 * np.random.standard_normal((V, 1))), "offs": striped(np.concatenate([np.random.permutation(V) for _ in range(-(-(N) // V))])[:N])}


def reference(table, w1, b1, w2, b2, w_out, b_out, offs):
    idx = offs[:16].T.reshape(-1)
    h1 = np.maximum(f64(w1).T @ f64(table)[idx].T + f64(b1), 0.0)
    h2 = np.maximum(f64(w2).T @ h1 + f64(b2), 0.0)
    return f64(w_out).T @ h2 + f64(b_out)

@@ -1,0 +1,107 @@
+import concourse.masks as masks
+import concourse.mybir as mybir
+
+BF16, F32, U16 = mybir.dt.bfloat16, mybir.dt.float32, mybir.dt.uint16
+RELU = mybir.ActivationFunctionType.Relu
+IDENTITY = mybir.ActivationFunctionType.Identity
+ADD, MAX = mybir.AluOpType.add, mybir.AluOpType.max
+
+P = 128
+V, D, H1, H2, N = 256, 128, 512, 256, 1024
+PIECE = V
+BANK = 512
+FLOPS = 2 * N * (D * H1 + H1 * H2 + H2 * V)
+
+
+def add_bias(nc, turn, result, sums, bias, relu):
+    if turn % 2 == 0:
+        nc.scalar.activation(result, sums, RELU if relu else IDENTITY, bias=bias)
+    elif relu:
+        nc.vector.tensor_scalar(result, sums, bias, 0.0, ADD, MAX)
+    else:
+        nc.vector.tensor_scalar(result, sums, bias, None, ADD)
+
+
+def tile_contextualmlpdecryptor_kernel(tc, table, w1, b1, w2, b2, w_out, b_out, offs, out):
+    nc = tc.nc
+    with (
+        tc.tile_pool(name="held", bufs=1) as held,
+        tc.tile_pool(name="logits", bufs=4) as logits,
+        tc.psum_pool(name="flip", bufs=1) as flip,
+        tc.psum_pool(name="banks", bufs=7) as banks,
+    ):
+        offsets = held.tile([P, N // 16], U16, name="offsets")
+        nc.sync.dma_start(offsets[:], offs)
+        rows = held.tile([P, V // P, D], BF16, name="rows")
+        nc.scalar.dma_start(rows[:], table.rearrange("(c p) d -> p c d", p=P))
+        w1_sb = held.tile([P, H1], BF16, name="w1_sb")
+        nc.sync.dma_start(w1_sb[:], w1)
+        b1_sb = held.tile([P, H1 // P], F32, name="b1_sb")
+        b2_sb = held.tile([P, H2 // P], F32, name="b2_sb")
+        b_out_sb = held.tile([P, V // P], F32, name="b_out_sb")
+        with nc.allow_non_contiguous_dma(reason="a bias a partition: 4-byte pieces, 1,024 in all"):
+            nc.scalar.dma_start(b1_sb[:], b1.rearrange("(k p) o -> p (k o)", p=P))
+            nc.scalar.dma_start(b2_sb[:], b2.rearrange("(k p) o -> p (k o)", p=P))
+            nc.scalar.dma_start(b_out_sb[:], b_out.rearrange("(k p) o -> p (k o)", p=P))
+        w2_sb = held.tile([P, H1 // P, H2], BF16, name="w2_sb")
+        nc.sync.dma_start(w2_sb[:], w2.rearrange("(k p) q -> p k q", p=P))
+        w_out_sb = held.tile([P, H2 // P, V], BF16, name="w_out_sb")
+        nc.sync.dma_start(w_out_sb[:], w_out.rearrange("(k p) v -> p k v", p=P))
+
+        identity = held.tile([P, P], BF16, name="identity")
+        masks.make_identity(nc, identity[:])
+        flipped = flip.tile([P, V], BF16, name="flipped")
+        for c in range(V // P):
+            nc.tensor.transpose(flipped[:, c * P : (c + 1) * P], rows[:, c, :], identity[:])
+        symbols = held.tile([P, V], BF16, name="symbols")
+        nc.vector.tensor_copy(symbols[:], flipped[:])
+
+        halves = range(N // BANK)
+        h1 = [held.tile([P, H1 // P, BANK], BF16, name=f"h1_{half}") for half in halves]
+        h2 = [held.tile([P, H2 // P, BANK], BF16, name=f"h2_{half}") for half in halves]
+        turn = 0
+
+        for half in halves:
+            for m in range(H1 // P):
+                sums = banks.tile([P, BANK], F32, name="sums")
+                for piece in range(BANK // PIECE):
+                    first = (half * BANK + piece * PIECE) // 16
+                    nc.tensor.matmul(
+                        sums[:, piece * PIECE : (piece + 1) * PIECE],
+                        w1_sb[:, m * P : (m + 1) * P],
+                        symbols[:].indirect(offsets[:, first : first + PIECE // 16]),
+                        start=True,
+                        stop=True,
+                    )
+                add_bias(nc, turn, h1[half][:, m, :], sums[:], b1_sb[:, m : m + 1], relu=True)
+                turn += 1
+
+        for half in halves:
+            for m in range(H2 // P):
+                sums = banks.tile([P, BANK], F32, name="sums")
+                for k in range(H1 // P):
+                    nc.tensor.matmul(
+                        sums[:],
+                        w2_sb[:, k, m * P : (m + 1) * P],
+                        h1[half][:, k, :],
+                        start=(k == 0),
+                        stop=(k == H1 // P - 1),
+                    )
+                add_bias(nc, turn, h2[half][:, m, :], sums[:], b2_sb[:, m : m + 1], relu=True)
+                turn += 1
+
+        for half in halves:
+            for m in range(V // P):
+                sums = banks.tile([P, BANK], F32, name="sums")
+                for k in range(H2 // P):
+                    nc.tensor.matmul(
+                        sums[:],
+                        w_out_sb[:, k, m * P : (m + 1) * P],
+                        h2[half][:, k, :],
+                        start=(k == 0),
+                        stop=(k == H2 // P - 1),
+                    )
+                block = logits.tile([P, BANK], F32, name="block")
+                add_bias(nc, turn, block[:], sums[:], b_out_sb[:, m : m + 1], relu=False)
+                turn += 1
+                nc.sync.dma_start(out[m * P : (m + 1) * P, half * BANK : (half + 1) * BANK], block[:])

@@ -10,6 +10,7 @@ P = 128
 V, D, H1, H2, N = 256, 128, 512, 256, 1024
 PIECE = V
 BANK = 512
+WARM_UP = 5
 FLOPS = 2 * N * (D * H1 + H1 * H2 + H2 * V)
 
 
@@ -47,6 +48,12 @@ def tile_contextualmlpdecryptor_kernel(tc, table, w1, b1, w2, b2, w_out, b_out, 
         nc.sync.dma_start(w2_sb[:], w2.rearrange("(k p) q -> p k q", p=P))
         w_out_sb = held.tile([P, H2 // P, V], BF16, name="w_out_sb")
         nc.sync.dma_start(w_out_sb[:], w_out.rearrange("(k p) v -> p k v", p=P))
+
+        zeros = held.tile([P, BANK], BF16, name="zeros")
+        nc.vector.memset(zeros[:], 0.0)
+        unread = banks.tile([P, BANK], F32, name="unread", tag="sums")
+        for repeat in range(WARM_UP):
+            nc.tensor.matmul(unread[:], zeros[:, :P], zeros[:], start=True, stop=True)
 
         identity = held.tile([P, P], BF16, name="identity")
         masks.make_identity(nc, identity[:])

@@ -10,7 +10,6 @@ P = 128
 V, D, H1, H2, N = 256, 128, 512, 256, 1024
 PIECE = V
 BANK = 512
-WARM_UP = 5
 FLOPS = 2 * N * (D * H1 + H1 * H2 + H2 * V)
 
 
@@ -27,7 +26,7 @@ def tile_contextualmlpdecryptor_kernel(tc, table, w1, b1, w2, b2, w_out, b_out, 
     nc = tc.nc
     with (
         tc.tile_pool(name="held", bufs=1) as held,
-        tc.tile_pool(name="logits", bufs=4) as logits,
+        tc.tile_pool(name="logits", bufs=6) as logits,
         tc.psum_pool(name="flip", bufs=1) as flip,
         tc.psum_pool(name="banks", bufs=7) as banks,
     ):
@@ -48,12 +47,6 @@ def tile_contextualmlpdecryptor_kernel(tc, table, w1, b1, w2, b2, w_out, b_out, 
         nc.sync.dma_start(w2_sb[:], w2.rearrange("(k p) q -> p k q", p=P))
         w_out_sb = held.tile([P, H2 // P, V], BF16, name="w_out_sb")
         nc.sync.dma_start(w_out_sb[:], w_out.rearrange("(k p) v -> p k v", p=P))
-
-        zeros = held.tile([P, BANK], BF16, name="zeros")
-        nc.vector.memset(zeros[:], 0.0)
-        unread = banks.tile([P, BANK], F32, name="unread", tag="sums")
-        for repeat in range(WARM_UP):
-            nc.tensor.matmul(unread[:], zeros[:, :P], zeros[:], start=True, stop=True)
 
         identity = held.tile([P, P], BF16, name="identity")
         masks.make_identity(nc, identity[:])
@@ -97,18 +90,19 @@ def tile_contextualmlpdecryptor_kernel(tc, table, w1, b1, w2, b2, w_out, b_out, 
                 add_bias(nc, turn, h2[half][:, m, :], sums[:], b2_sb[:, m : m + 1], relu=True)
                 turn += 1
 
-        for half in halves:
+        for first, width in ((0, BANK), (BANK, BANK // 2), (BANK + BANK // 2, BANK // 2)):
+            half, start = first // BANK, first % BANK
             for m in range(V // P):
                 sums = banks.tile([P, BANK], F32, name="sums")
                 for k in range(H2 // P):
                     nc.tensor.matmul(
-                        sums[:],
+                        sums[:, :width],
                         w_out_sb[:, k, m * P : (m + 1) * P],
-                        h2[half][:, k, :],
+                        h2[half][:, k, start : start + width],
                         start=(k == 0),
                         stop=(k == H2 // P - 1),
                     )
                 block = logits.tile([P, BANK], F32, name="block")
-                add_bias(nc, turn, block[:], sums[:], b_out_sb[:, m : m + 1], relu=False)
+                add_bias(nc, turn, block[:, :width], sums[:, :width], b_out_sb[:, m : m + 1], relu=False)
                 turn += 1
-                nc.sync.dma_start(out[m * P : (m + 1) * P, half * BANK : (half + 1) * BANK], block[:])
+                nc.sync.dma_start(out[m * P : (m + 1) * P, first : first + width], block[:, :width])

@@ -10,6 +10,7 @@ P = 128
 V, D, H1, H2, N = 256, 128, 512, 256, 1024
 PIECE = V
 BANK = 512
+QUARTER = 256
 FLOPS = 2 * N * (D * H1 + H1 * H2 + H2 * V)
 
 
@@ -26,7 +27,7 @@ def tile_contextualmlpdecryptor_kernel(tc, table, w1, b1, w2, b2, w_out, b_out, 
     nc = tc.nc
     with (
         tc.tile_pool(name="held", bufs=1) as held,
-        tc.tile_pool(name="logits", bufs=6) as logits,
+        tc.tile_pool(name="logits", bufs=8) as logits,
         tc.psum_pool(name="flip", bufs=1) as flip,
         tc.psum_pool(name="banks", bufs=7) as banks,
     ):
@@ -58,7 +59,6 @@ def tile_contextualmlpdecryptor_kernel(tc, table, w1, b1, w2, b2, w_out, b_out, 
 
         halves = range(N // BANK)
         h1 = [held.tile([P, H1 // P, BANK], BF16, name=f"h1_{half}") for half in halves]
-        h2 = [held.tile([P, H2 // P, BANK], BF16, name=f"h2_{half}") for half in halves]
         turn = 0
 
         for half in halves:
@@ -76,33 +76,36 @@ def tile_contextualmlpdecryptor_kernel(tc, table, w1, b1, w2, b2, w_out, b_out, 
                 add_bias(nc, turn, h1[half][:, m, :], sums[:], b1_sb[:, m : m + 1], relu=True)
                 turn += 1
 
-        for half in halves:
-            for m in range(H2 // P):
-                sums = banks.tile([P, BANK], F32, name="sums")
-                for k in range(H1 // P):
-                    nc.tensor.matmul(
-                        sums[:],
-                        w2_sb[:, k, m * P : (m + 1) * P],
-                        h1[half][:, k, :],
-                        start=(k == 0),
-                        stop=(k == H1 // P - 1),
-                    )
-                add_bias(nc, turn, h2[half][:, m, :], sums[:], b2_sb[:, m : m + 1], relu=True)
-                turn += 1
-
-        for first, width in ((0, BANK), (BANK, BANK // 2), (BANK + BANK // 2, BANK // 2)):
-            half, start = first // BANK, first % BANK
-            for m in range(V // P):
-                sums = banks.tile([P, BANK], F32, name="sums")
-                for k in range(H2 // P):
-                    nc.tensor.matmul(
-                        sums[:, :width],
-                        w_out_sb[:, k, m * P : (m + 1) * P],
-                        h2[half][:, k, start : start + width],
-                        start=(k == 0),
-                        stop=(k == H2 // P - 1),
-                    )
-                block = logits.tile([P, BANK], F32, name="block")
-                add_bias(nc, turn, block[:, :width], sums[:, :width], b_out_sb[:, m : m + 1], relu=False)
-                turn += 1
-                nc.sync.dma_start(out[m * P : (m + 1) * P, first : first + width], block[:, :width])
+        quarters = N // QUARTER
+        h2 = [held.tile([P, H2 // P, QUARTER], BF16, name=f"h2_{q}") for q in range(quarters)]
+        for step in range(quarters + 1):
+            if step < quarters:
+                half, start = (step * QUARTER) // BANK, (step * QUARTER) % BANK
+                for m in range(H2 // P):
+                    sums = banks.tile([P, BANK], F32, name="sums")
+                    for k in range(H1 // P):
+                        nc.tensor.matmul(
+                            sums[:, :QUARTER],
+                            w2_sb[:, k, m * P : (m + 1) * P],
+                            h1[half][:, k, start : start + QUARTER],
+                            start=(k == 0),
+                            stop=(k == H1 // P - 1),
+                        )
+                    add_bias(nc, turn, h2[step][:, m, :], sums[:, :QUARTER], b2_sb[:, m : m + 1], relu=True)
+                    turn += 1
+            if step > 0:
+                q = step - 1
+                for m in range(V // P):
+                    sums = banks.tile([P, BANK], F32, name="sums")
+                    for k in range(H2 // P):
+                        nc.tensor.matmul(
+                            sums[:, :QUARTER],
+                            w_out_sb[:, k, m * P : (m + 1) * P],
+                            h2[q][:, k, :],
+                            start=(k == 0),
+                            stop=(k == H2 // P - 1),
+                        )
+                    block = logits.tile([P, QUARTER], F32, name="block")
+                    add_bias(nc, turn, block[:], sums[:, :QUARTER], b_out_sb[:, m : m + 1], relu=False)
+                    turn += 1
+                    nc.sync.dma_start(out[m * P : (m + 1) * P, q * QUARTER : (q + 1) * QUARTER], block[:])

@@ -50,7 +50,8 @@ def tile_contextualmlpdecryptor_kernel(tc, table, w1, b1, w2, b2, w_out, b_out, 
         nc.sync.dma_start(w_out_sb[:], w_out.rearrange("(k p) v -> p k v", p=P))
 
         identity = held.tile([P, P], BF16, name="identity")
-        masks.make_identity(nc, identity[:])
+        nc.vector.memset(identity[:], 0.0)
+        masks.make_identity(nc, identity[:], nomemset=True)
         flipped = flip.tile([P, V], BF16, name="flipped")
         for c in range(V // P):
             nc.tensor.transpose(flipped[:, c * P : (c + 1) * P], rows[:, c, :], identity[:])

import concourse.masks as masks
import concourse.mybir as mybir

BF16, F32, U16 = mybir.dt.bfloat16, mybir.dt.float32, mybir.dt.uint16
RELU = mybir.ActivationFunctionType.Relu
IDENTITY = mybir.ActivationFunctionType.Identity
ADD, MAX = mybir.AluOpType.add, mybir.AluOpType.max

P = 128
V, D, H1, H2, N = 256, 128, 512, 256, 1024
PIECE = V
BANK = 512
QUARTER = 256
FLOPS = 2 * N * (D * H1 + H1 * H2 + H2 * V)


def add_bias(nc, turn, result, sums, bias, relu):
    if turn % 2 == 0:
        nc.scalar.activation(result, sums, RELU if relu else IDENTITY, bias=bias)
    elif relu:
        nc.vector.tensor_scalar(result, sums, bias, 0.0, ADD, MAX)
    else:
        nc.vector.tensor_scalar(result, sums, bias, None, ADD)


def tile_contextualmlpdecryptor_kernel(tc, table, w1, b1, w2, b2, w_out, b_out, offs, out):
    nc = tc.nc
    with (
        tc.tile_pool(name="held", bufs=1) as held,
        tc.tile_pool(name="logits", bufs=8) as logits,
        tc.psum_pool(name="flip", bufs=1) as flip,
        tc.psum_pool(name="banks", bufs=7) as banks,
    ):
        offsets = held.tile([P, N // 16], U16, name="offsets")
        nc.sync.dma_start(offsets[:], offs)
        rows = held.tile([P, V // P, D], BF16, name="rows")
        nc.scalar.dma_start(rows[:], table.rearrange("(c p) d -> p c d", p=P))
        w1_sb = held.tile([P, H1], BF16, name="w1_sb")
        nc.sync.dma_start(w1_sb[:], w1)
        b1_sb = held.tile([P, H1 // P], F32, name="b1_sb")
        b2_sb = held.tile([P, H2 // P], F32, name="b2_sb")
        b_out_sb = held.tile([P, V // P], F32, name="b_out_sb")
        with nc.allow_non_contiguous_dma(reason="a bias a partition: 4-byte pieces, 1,024 in all"):
            nc.scalar.dma_start(b1_sb[:], b1.rearrange("(k p) o -> p (k o)", p=P))
            nc.scalar.dma_start(b2_sb[:], b2.rearrange("(k p) o -> p (k o)", p=P))
            nc.scalar.dma_start(b_out_sb[:], b_out.rearrange("(k p) o -> p (k o)", p=P))
        w2_sb = held.tile([P, H1 // P, H2], BF16, name="w2_sb")
        nc.sync.dma_start(w2_sb[:], w2.rearrange("(k p) q -> p k q", p=P))
        w_out_sb = held.tile([P, H2 // P, V], BF16, name="w_out_sb")
        nc.sync.dma_start(w_out_sb[:], w_out.rearrange("(k p) v -> p k v", p=P))

        identity = held.tile([P, P], BF16, name="identity")
        nc.vector.memset(identity[:], 0.0)
        masks.make_identity(nc, identity[:], nomemset=True)
        flipped = flip.tile([P, V], BF16, name="flipped")
        for c in range(V // P):
            nc.tensor.transpose(flipped[:, c * P : (c + 1) * P], rows[:, c, :], identity[:])
        symbols = held.tile([P, V], BF16, name="symbols")
        nc.vector.tensor_copy(symbols[:], flipped[:])

        halves = range(N // BANK)
        h1 = [held.tile([P, H1 // P, BANK], BF16, name=f"h1_{half}") for half in halves]
        turn = 0

        for half in halves:
            for m in range(H1 // P):
                sums = banks.tile([P, BANK], F32, name="sums")
                for piece in range(BANK // PIECE):
                    first = (half * BANK + piece * PIECE) // 16
                    nc.tensor.matmul(
                        sums[:, piece * PIECE : (piece + 1) * PIECE],
                        w1_sb[:, m * P : (m + 1) * P],
                        symbols[:].indirect(offsets[:, first : first + PIECE // 16]),
                        start=True,
                        stop=True,
                    )
                add_bias(nc, turn, h1[half][:, m, :], sums[:], b1_sb[:, m : m + 1], relu=True)
                turn += 1

        quarters = N // QUARTER
        h2 = [held.tile([P, H2 // P, QUARTER], BF16, name=f"h2_{q}") for q in range(quarters)]
        for step in range(quarters + 1):
            if step < quarters:
                half, start = (step * QUARTER) // BANK, (step * QUARTER) % BANK
                for m in range(H2 // P):
                    sums = banks.tile([P, BANK], F32, name="sums")
                    for k in range(H1 // P):
                        nc.tensor.matmul(
                            sums[:, :QUARTER],
                            w2_sb[:, k, m * P : (m + 1) * P],
                            h1[half][:, k, start : start + QUARTER],
                            start=(k == 0),
                            stop=(k == H1 // P - 1),
                        )
                    add_bias(nc, turn, h2[step][:, m, :], sums[:, :QUARTER], b2_sb[:, m : m + 1], relu=True)
                    turn += 1
            if step > 0:
                q = step - 1
                for m in range(V // P):
                    sums = banks.tile([P, BANK], F32, name="sums")
                    for k in range(H2 // P):
                        nc.tensor.matmul(
                            sums[:, :QUARTER],
                            w_out_sb[:, k, m * P : (m + 1) * P],
                            h2[q][:, k, :],
                            start=(k == 0),
                            stop=(k == H2 // P - 1),
                        )
                    block = logits.tile([P, QUARTER], F32, name="block")
                    add_bias(nc, turn, block[:], sums[:, :QUARTER], b_out_sb[:, m : m + 1], relu=False)
                    turn += 1
                    nc.sync.dma_start(out[m * P : (m + 1) * P, q * QUARTER : (q + 1) * QUARTER], block[:])
